import numpy as np
import ml_dtypes


def mxq(x, axis, fmt="e4m3"):
    dtype, down = {"e4m3": (ml_dtypes.float8_e4m3fn, 7), "e5m2": (ml_dtypes.float8_e5m2, 14)}[fmt]
    v = np.moveaxis(np.asarray(x, np.float32).astype(ml_dtypes.bfloat16).astype(np.float64), axis, -1)
    blocks = v.reshape(v.shape[:-1] + (-1, 32))
    amax = np.abs(blocks).max(-1, keepdims=True)
    byte = np.maximum(np.where(amax > 0, np.frexp(amax)[1] - 1 + 127, 0) - down, 1)
    scale = np.exp2(byte - 127.0)
    codes = (blocks / scale).astype(np.float32).astype(dtype).astype(np.float64)
    return np.moveaxis((codes * scale).reshape(v.shape), -1, axis)


WIDE = False


def mx_kscale(k):
    if not WIDE:
        return np.ones(k)
    levels = np.array([10, -10, 5, -5, 0])
    if k % 512:
        return np.exp2(np.random.permutation(np.resize(levels, k // 32))).repeat(32)
    a = np.empty((k // 512, 16))
    for p in range(k // 512):
        a[p, :8] = np.random.permutation(np.resize(levels, 8))
        for g in range(8):
            far = levels[np.abs(levels - a[p, g]) >= 10]
            a[p, g + 8] = far[np.random.randint(len(far))]
    return np.exp2(a.ravel()).repeat(32)


BF16 = ml_dtypes.bfloat16


def bf(x):
    return np.asarray(x, np.float32).astype(BF16)


def f64(x):
    return np.asarray(x).astype(np.float64)


B, N, C = 2, 512, 1024
R = B * N
G = 3 * C
DENS = 0.1


def setup_inputs():
    s, t = mx_kscale(N), mx_kscale(C)
    edge = np.random.random((B, N, N)) < DENS
    weights = np.where(edge, np.random.random((B, N, N)), 0.0) / np.sqrt(DENS * N / 3.0)
    return {"adjacent": bf(weights * s),
            "annotations": bf(np.random.standard_normal((B, N, C)) / s[:, None] * t),
            "gc_bias": bf(np.random.standard_normal((1, 1, C)) * 0.3 * t),
            "kernel": bf(np.random.standard_normal((C, G)) / np.sqrt(C) / t[:, None]),
            "bias_x": bf(np.random.standard_normal(G) * 0.3)}


def reference(adjacent, annotations, gc_bias, kernel, bias_x):
    a = f64(adjacent)
    v = f64(bf(mxq(a, a.ndim - 1, "e4m3") @ mxq(f64(annotations), 1, "e4m3"))) + f64(gc_bias)
    x = v.reshape(-1, v.shape[-1])
    return (mxq(x, 1, "e4m3") @ mxq(f64(kernel), 0, "e4m3")) + f64(bias_x)

@@ -1,0 +1,265 @@
+from contextlib import ExitStack
+
+import concourse.mybir as mybir
+from concourse.masks import make_identity
+
+F32 = mybir.dt.float32
+BF16 = mybir.dt.bfloat16
+U32 = mybir.dt.uint32
+U8 = mybir.dt.uint8
+FP8X4 = mybir.dt.float8_e4m3fn_x4
+ADD = mybir.AluOpType.add
+
+BANK_DT = BF16
+
+P = 128
+B, N, C, G = 2, 512, 1024, 3072
+FLOPS = 2 * B * N * N * C + 2 * B * N * C * G
+
+NIT = N // P
+NRT = B * NIT
+NG2 = C // 512
+CW = 1024
+NCW = G // CW
+NH = CW // 512
+
+
+def tile_gatedgraphconvolution_pa_kernel(tc, adjacent, annotations, gc_bias, kernel, bias_x, out):
+    nc = tc.nc
+    with ExitStack() as ctx:
+        keep = ctx.enter_context(tc.tile_pool(name="keep", bufs=1))
+        kgp = ctx.enter_context(tc.tile_pool(name="kgp", bufs=4))
+        osb = ctx.enter_context(tc.tile_pool(name="osb", bufs=6))
+        ps_tr = ctx.enter_context(tc.psum_pool(name="ps_tr", bufs=2))
+        ps_s1 = ctx.enter_context(tc.psum_pool(name="ps_s1", bufs=2))
+        ps_s2 = ctx.enter_context(tc.psum_pool(name="ps_s2", bufs=4))
+        ctx.enter_context(tc.manual_schedule())
+
+        warm_in = keep.tile([P, 8], F32, name="warm_in")
+        warm_out = keep.tile([P, 8], F32, name="warm_out")
+        nc.vector.memset(warm_in[:], 0.0)
+        nc.scalar.copy(out=warm_out[:], in_=warm_in[:])
+
+        ident = keep.tile([P, P], F32, name="ident")
+        make_identity(nc, ident[:])
+
+        x_raw = [keep.tile([P, 4, C], BF16, name="x_raw%d" % b) for b in range(B)]
+        a_raw = [keep.tile([P, NIT, N], BF16, name="a_raw%d" % b) for b in range(B)]
+        k_raw = [[keep.tile([P, 4, CW], BF16, name="k_raw%d_%d" % (cw, g)) for g in range(NG2)] for cw in range(NCW)]
+        gcb = keep.tile([P, NG2, 4], BF16, name="gcb")
+        bx = keep.tile([P, G], BF16, name="bx")
+
+        x_grp = [keep.tile([P, C, 4], BF16, name="x_grp%d" % b, align_bytes=64) for b in range(B)]
+        x_cod = [keep.tile([P, C], U32, name="x_cod%d" % b, align_bytes=64) for b in range(B)]
+        x_scl = [keep.tile([P, C], U8, name="x_scl%d" % b, align_bytes=64) for b in range(B)]
+        a_grp = [keep.tile([P, N, 4], BF16, name="a_grp%d" % b, align_bytes=64) for b in range(B)]
+        a_cod = [keep.tile([P, N], U32, name="a_cod%d" % b, align_bytes=64) for b in range(B)]
+        a_scl = [keep.tile([P, N], U8, name="a_scl%d" % b, align_bytes=64) for b in range(B)]
+        v_grp = [keep.tile([P, NG2, P, 4], BF16, name="v_grp%d" % r, align_bytes=64) for r in range(NRT)]
+        v_cod = [keep.tile([P, NG2, P], U32, name="v_cod%d" % r, align_bytes=64) for r in range(NRT)]
+        v_scl = [keep.tile([P, NG2, P], U8, name="v_scl%d" % r, align_bytes=64) for r in range(NRT)]
+        k_cod = [keep.tile([P, NG2, CW], U32, name="k_cod%d" % cw, align_bytes=64) for cw in range(NCW)]
+        k_scl = [keep.tile([P, NG2, CW], U8, name="k_scl%d" % cw, align_bytes=64) for cw in range(NCW)]
+
+        out_v = out.rearrange("(b m i) g -> b i m g", b=B, i=NIT)
+        k_v = kernel.rearrange("(g p j) w -> g p j w", g=NG2, j=4)
+
+        def load_x(b):
+            nc.sync.dma_start(out=x_raw[b][:], in_=annotations[b].rearrange("(p j) c -> p j c", j=4))
+
+        def load_a(b):
+            nc.sync.dma_start(out=a_raw[b][:], in_=adjacent[b].rearrange("(p i) j -> p i j", i=NIT))
+
+        def load_k(cw, g):
+            nc.sync.dma_start(out=k_raw[cw][g][:], in_=k_v[g, :, :, cw * CW : (cw + 1) * CW])
+
+        nc.scalar.dma_start(out=gcb[:], in_=gc_bias[0, 0, :].rearrange("(g p t) -> p g t", g=NG2, t=4))
+        load_x(0)
+        load_a(0)
+        load_a(1)
+        load_x(1)
+        load_k(0, 0)
+        load_k(0, 1)
+        nc.sync.dma_start(out=bx[:], in_=bias_x.partition_broadcast(P))
+        for cw in range(1, NCW):
+            for g in range(NG2):
+                load_k(cw, g)
+
+        def copy_on(eng, dst, src):
+            if eng == "v":
+                nc.vector.tensor_copy(out=dst, in_=src)
+            else:
+                nc.scalar.copy(out=dst, in_=src)
+
+        def x_il(b, g, eng):
+            cols = slice(g * 512, (g + 1) * 512)
+            copy_on(
+                eng,
+                x_grp[b][:, cols, :].rearrange("p (t m) j -> p t m j", t=4),
+                x_raw[b][:, :, cols].rearrange("p j (m t) -> p t m j", t=4),
+            )
+
+        def x_q(b, g):
+            cols = slice(g * 512, (g + 1) * 512)
+            nc.vector.quantize_mx(
+                out=x_cod[b][:, cols].bitcast(FP8X4),
+                scales=x_scl[b][:, cols],
+                in_=x_grp[b][:, cols, :].rearrange("p c j -> p (c j)"),
+            )
+
+        tr_tiles = {}
+
+        def a_tr(b, s):
+            tr = ps_tr.tile([P, 2, 2, P], F32, name="tr")
+            tr_tiles[(b, s)] = tr
+            for e in range(2):
+                words = a_raw[b][:, 2 * s + e, :].bitcast(F32)
+                for u in range(2):
+                    nc.tensor.transpose(tr[:, e, u, :], words[:, u : N // 2 : 2], ident[:])
+
+        def a_cp(b, s, eng):
+            tr = tr_tiles[(b, s)]
+            dst = a_grp[b][:, 2 * s * P : (2 * s + 2) * P, :].rearrange("p n t -> p (n t)").bitcast(F32)
+            copy_on(
+                eng,
+                dst.rearrange("p (e r u) -> p e r u", e=2, u=2),
+                tr[:].rearrange("p e u r -> p e r u"),
+            )
+
+        def a_q(b):
+            nc.vector.quantize_mx(
+                out=a_cod[b][:].bitcast(FP8X4),
+                scales=a_scl[b][:],
+                in_=a_grp[b][:].rearrange("p n t -> p (n t)"),
+            )
+
+        s1_tiles = {}
+
+        def s1_mm(r, g):
+            b, it = r // NIT, r % NIT
+            s1 = ps_s1.tile([P, 4, P], BANK_DT, name="s1")
+            s1_tiles[(r, g)] = s1
+            rows = slice(it * P, (it + 1) * P)
+            for t in range(4):
+                cols = slice(g * 512 + t * P, g * 512 + (t + 1) * P)
+                nc.tensor.matmul_mx(
+                    out=s1[:, t, :],
+                    lhsT=x_cod[b][:, cols].bitcast(FP8X4),
+                    lhsT_scale=x_scl[b][:, cols],
+                    rhs=a_cod[b][:, rows].bitcast(FP8X4),
+                    rhs_scale=a_scl[b][:, rows],
+                    start=True,
+                    stop=True,
+                )
+
+        def s1_out(r, g):
+            nc.vector.tensor_tensor(
+                out=v_grp[r][:, g, :, :],
+                in0=s1_tiles[(r, g)][:].rearrange("p t n -> p n t"),
+                in1=gcb[:, g, :].unsqueeze(1).to_broadcast([P, P, 4]),
+                op=ADD,
+            )
+
+        def v_q(r):
+            nc.vector.quantize_mx(
+                out=v_cod[r][:].rearrange("p g n -> p (g n)").bitcast(FP8X4),
+                scales=v_scl[r][:].rearrange("p g n -> p (g n)"),
+                in_=v_grp[r][:].rearrange("p g n t -> p (g n t)"),
+            )
+
+        kg_tiles = {}
+
+        def k_il(cw, h, g, eng):
+            kg = kgp.tile([P, 512, 4], BF16, name="kg", align_bytes=64)
+            kg_tiles[(cw, h, g)] = kg
+            copy_on(eng, kg[:], k_raw[cw][g][:, :, h * 512 : (h + 1) * 512].rearrange("p j w -> p w j"))
+
+        def k_q(cw, h, g):
+            cols = slice(h * 512, (h + 1) * 512)
+            nc.vector.quantize_mx(
+                out=k_cod[cw][:, g, cols].bitcast(FP8X4),
+                scales=k_scl[cw][:, g, cols],
+                in_=kg_tiles[(cw, h, g)][:].rearrange("p w j -> p (w j)"),
+            )
+
+        s2_tiles = {}
+
+        def s2_mm(cw, r):
+            for h in range(NH):
+                acc = ps_s2.tile([P, 512], F32, name="acc")
+                s2_tiles[(cw, r, h)] = acc
+                cols = slice(h * 512, (h + 1) * 512)
+                for g in range(NG2):
+                    nc.tensor.matmul_mx(
+                        out=acc[:],
+                        lhsT=v_cod[r][:, g, :].bitcast(FP8X4),
+                        lhsT_scale=v_scl[r][:, g, :],
+                        rhs=k_cod[cw][:, g, cols].bitcast(FP8X4),
+                        rhs_scale=k_scl[cw][:, g, cols],
+                        start=(g == 0),
+                        stop=(g == NG2 - 1),
+                    )
+
+        def s2_out(cw, r):
+            b, it = r // NIT, r % NIT
+            o = osb.tile([P, CW], F32, name="o")
+            for h in range(NH):
+                nc.vector.tensor_tensor(
+                    out=o[:, h * 512 : (h + 1) * 512],
+                    in0=s2_tiles[(cw, r, h)][:],
+                    in1=bx[:, cw * CW + h * 512 : cw * CW + (h + 1) * 512],
+                    op=ADD,
+                )
+            nc.sync.dma_start(out=out_v[b, it, :, cw * CW : (cw + 1) * CW], in_=o[:])
+
+
+        pieces = [(cw, h, g) for cw in range(NCW) for h in range(NH) for g in range(NG2)]
+        units1 = [(r, g) for r in range(NRT) for g in range(NG2)]
+        units2 = [(cw, r) for cw in range(NCW) for r in range(NRT)]
+        KGB = 4
+
+        def k_q_then_il(j):
+            k_q(*pieces[j])
+            if j + KGB < len(pieces):
+                k_il(*pieces[j + KGB], "s")
+
+        x_il(0, 0, "v")
+        x_il(0, 1, "s")
+        a_tr(0, 0)
+        a_tr(0, 1)
+        x_q(0, 0)
+        a_cp(0, 0, "v")
+        a_cp(0, 1, "v")
+        a_tr(1, 0)
+        a_tr(1, 1)
+        a_cp(1, 0, "s")
+        a_cp(1, 1, "s")
+        x_q(0, 1)
+        a_q(0)
+        a_q(1)
+        x_il(1, 0, "v")
+        x_il(1, 1, "s")
+        for j in range(KGB):
+            k_il(*pieces[j], "s")
+
+        extra1 = {1: lambda: x_q(1, 0), 4: lambda: x_q(1, 1), 8: lambda: k_q_then_il(0), 10: lambda: k_q_then_il(1), 12: lambda: k_q_then_il(2), 14: lambda: k_q_then_il(3)}
+        s1_mm(*units1[0])
+        for i in range(len(units1)):
+            r, g = units1[i]
+            if i in extra1:
+                extra1[i]()
+            if i + 1 < len(units1):
+                s1_mm(*units1[i + 1])
+            s1_out(r, g)
+            if g == 1 and r >= 1:
+                v_q(r - 1)
+        v_q(NRT - 1)
+
+        s2_mm(*units2[0])
+        for i in range(len(units2)):
+            cw, r = units2[i]
+            if i + 1 < len(units2):
+                s2_mm(*units2[i + 1])
+            s2_out(cw, r)
+            if cw + 1 < NCW and r % 2 == 0:
+                k_q_then_il(4 * (cw + 1) + r // 2)

@@ -172,7 +172,11 @@ def tile_gatedgraphconvolution_pa_kernel(tc, adjacent, annotations, gc_bias, ker
         def k_il(cw, h, g, eng):
             kg = kgp.tile([P, 512, 4], BF16, name="kg", align_bytes=64)
             kg_tiles[(cw, h, g)] = kg
-            copy_on(eng, kg[:], k_raw[cw][g][:, :, h * 512 : (h + 1) * 512].rearrange("p j w -> p w j"))
+            copy_on(
+                eng,
+                kg[:].rearrange("p (c i) j -> p c j i", i=4),
+                k_raw[cw][g][:, :, h * 512 : (h + 1) * 512].rearrange("p j (c i) -> p c j i", i=4),
+            )
 
         def k_q(cw, h, g):
             cols = slice(h * 512, (h + 1) * 512)

@@ -9,8 +9,7 @@ U32 = mybir.dt.uint32
 U8 = mybir.dt.uint8
 FP8X4 = mybir.dt.float8_e4m3fn_x4
 ADD = mybir.AluOpType.add
-
-BANK_DT = BF16
+MULT = mybir.AluOpType.mult
 
 P = 128
 B, N, C, G = 2, 512, 1024, 3072
@@ -22,17 +21,18 @@ NG2 = C // 512
 CW = 1024
 NCW = G // CW
 NH = CW // 512
+NCH = G // 512
+VQ = 2
 
 
 def tile_gatedgraphconvolution_pa_kernel(tc, adjacent, annotations, gc_bias, kernel, bias_x, out):
     nc = tc.nc
     with ExitStack() as ctx:
         keep = ctx.enter_context(tc.tile_pool(name="keep", bufs=1))
-        kgp = ctx.enter_context(tc.tile_pool(name="kgp", bufs=4))
-        osb = ctx.enter_context(tc.tile_pool(name="osb", bufs=6))
-        ps_tr = ctx.enter_context(tc.psum_pool(name="ps_tr", bufs=2))
-        ps_s1 = ctx.enter_context(tc.psum_pool(name="ps_s1", bufs=2))
-        ps_s2 = ctx.enter_context(tc.psum_pool(name="ps_s2", bufs=4))
+        kgp = ctx.enter_context(tc.tile_pool(name="kgp", bufs=2))
+        vrp = ctx.enter_context(tc.tile_pool(name="vrp", bufs=4))
+        osb = ctx.enter_context(tc.tile_pool(name="osb", bufs=8))
+        psum = ctx.enter_context(tc.psum_pool(name="psum", bufs=8))
         ctx.enter_context(tc.manual_schedule())
 
         warm_in = keep.tile([P, 8], F32, name="warm_in")
@@ -46,7 +46,7 @@ def tile_gatedgraphconvolution_pa_kernel(tc, adjacent, annotations, gc_bias, ker
         x_raw = [keep.tile([P, 4, C], BF16, name="x_raw%d" % b) for b in range(B)]
         a_raw = [keep.tile([P, NIT, N], BF16, name="a_raw%d" % b) for b in range(B)]
         k_raw = [[keep.tile([P, 4, CW], BF16, name="k_raw%d_%d" % (cw, g)) for g in range(NG2)] for cw in range(NCW)]
-        gcb = keep.tile([P, NG2, 4], BF16, name="gcb")
+        gcbb = keep.tile([P, C], BF16, name="gcbb")
         bx = keep.tile([P, G], BF16, name="bx")
 
         x_grp = [keep.tile([P, C, 4], BF16, name="x_grp%d" % b, align_bytes=64) for b in range(B)]
@@ -55,17 +55,17 @@ def tile_gatedgraphconvolution_pa_kernel(tc, adjacent, annotations, gc_bias, ker
         a_grp = [keep.tile([P, N, 4], BF16, name="a_grp%d" % b, align_bytes=64) for b in range(B)]
         a_cod = [keep.tile([P, N], U32, name="a_cod%d" % b, align_bytes=64) for b in range(B)]
         a_scl = [keep.tile([P, N], U8, name="a_scl%d" % b, align_bytes=64) for b in range(B)]
-        v_grp = [keep.tile([P, NG2, P, 4], BF16, name="v_grp%d" % r, align_bytes=64) for r in range(NRT)]
-        v_cod = [keep.tile([P, NG2, P], U32, name="v_cod%d" % r, align_bytes=64) for r in range(NRT)]
-        v_scl = [keep.tile([P, NG2, P], U8, name="v_scl%d" % r, align_bytes=64) for r in range(NRT)]
-        k_cod = [keep.tile([P, NG2, CW], U32, name="k_cod%d" % cw, align_bytes=64) for cw in range(NCW)]
-        k_scl = [keep.tile([P, NG2, CW], U8, name="k_scl%d" % cw, align_bytes=64) for cw in range(NCW)]
+        v_grp = [keep.tile([P, VQ, NG2, P, 4], BF16, name="v_grp%d" % q, align_bytes=64) for q in range(NRT // VQ)]
+        v_cod = [keep.tile([P, VQ, NG2, P], U32, name="v_cod%d" % q, align_bytes=64) for q in range(NRT // VQ)]
+        v_scl = [keep.tile([P, VQ, NG2, P], U8, name="v_scl%d" % q, align_bytes=64) for q in range(NRT // VQ)]
+        k_cod = [keep.tile([P, NG2, 512], U32, name="k_cod%d" % c, align_bytes=64) for c in range(NCH)]
+        k_scl = [keep.tile([P, NG2, 512], U8, name="k_scl%d" % c, align_bytes=64) for c in range(NCH)]
 
         out_v = out.rearrange("(b m i) g -> b i m g", b=B, i=NIT)
         k_v = kernel.rearrange("(g p j) w -> g p j w", g=NG2, j=4)
 
-        def load_x(b):
-            nc.sync.dma_start(out=x_raw[b][:], in_=annotations[b].rearrange("(p j) c -> p j c", j=4))
+        def load_x(b, lo, hi):
+            nc.sync.dma_start(out=x_raw[b][:, :, lo:hi], in_=annotations[b].rearrange("(p j) c -> p j c", j=4)[:, :, lo:hi])
 
         def load_a(b):
             nc.sync.dma_start(out=a_raw[b][:], in_=adjacent[b].rearrange("(p i) j -> p i j", i=NIT))
@@ -73,44 +73,53 @@ def tile_gatedgraphconvolution_pa_kernel(tc, adjacent, annotations, gc_bias, ker
         def load_k(cw, g):
             nc.sync.dma_start(out=k_raw[cw][g][:], in_=k_v[g, :, :, cw * CW : (cw + 1) * CW])
 
-        nc.scalar.dma_start(out=gcb[:], in_=gc_bias[0, 0, :].rearrange("(g p t) -> p g t", g=NG2, t=4))
-        load_x(0)
+        def load_k_half(cw, g, h):
+            nc.sync.dma_start(
+                out=k_raw[cw][g][:, :, h * 512 : (h + 1) * 512],
+                in_=k_v[g, :, :, cw * CW + h * 512 : cw * CW + (h + 1) * 512],
+            )
+
+        load_x(0, 0, 256)
+        load_x(0, 256, 512)
+        load_x(0, 512, 1024)
         load_a(0)
+        load_x(1, 0, 1024)
+        nc.sync.dma_start(out=gcbb[:], in_=gc_bias[0, 0, :].partition_broadcast(P))
         load_a(1)
-        load_x(1)
-        load_k(0, 0)
-        load_k(0, 1)
+        for h in range(NH):
+            for g in range(NG2):
+                load_k_half(0, g, h)
         nc.sync.dma_start(out=bx[:], in_=bias_x.partition_broadcast(P))
         for cw in range(1, NCW):
             for g in range(NG2):
                 load_k(cw, g)
 
-        def copy_on(eng, dst, src):
+        def il_on(eng, dst, src):
             if eng == "v":
-                nc.vector.tensor_copy(out=dst, in_=src)
+                nc.vector.tensor_copy(out=dst, in_=src.rearrange("p j w -> p w j"))
+            elif eng == "s":
+                nc.scalar.copy(
+                    out=dst.rearrange("p (c i) j -> p c j i", i=4), in_=src.rearrange("p j (c i) -> p c j i", i=4)
+                )
             else:
-                nc.scalar.copy(out=dst, in_=src)
+                nc.gpsimd.tensor_scalar(
+                    out=dst, in0=src.rearrange("p j w -> p w j"), scalar1=1.0, scalar2=0.0, op0=MULT, op1=ADD
+                )
 
-        def x_il(b, g, eng):
-            cols = slice(g * 512, (g + 1) * 512)
-            copy_on(
-                eng,
-                x_grp[b][:, cols, :].rearrange("p (t m) j -> p t m j", t=4),
-                x_raw[b][:, :, cols].rearrange("p j (m t) -> p t m j", t=4),
-            )
+        def x_il(b, lo, hi, eng):
+            il_on(eng, x_grp[b][:, lo:hi, :], x_raw[b][:, :, lo:hi])
 
-        def x_q(b, g):
-            cols = slice(g * 512, (g + 1) * 512)
+        def x_q(b, lo, hi):
             nc.vector.quantize_mx(
-                out=x_cod[b][:, cols].bitcast(FP8X4),
-                scales=x_scl[b][:, cols],
-                in_=x_grp[b][:, cols, :].rearrange("p c j -> p (c j)"),
+                out=x_cod[b][:, lo:hi].bitcast(FP8X4),
+                scales=x_scl[b][:, lo:hi],
+                in_=x_grp[b][:, lo:hi, :].rearrange("p c j -> p (c j)"),
             )
 
         tr_tiles = {}
 
         def a_tr(b, s):
-            tr = ps_tr.tile([P, 2, 2, P], F32, name="tr")
+            tr = psum.tile([P, 2, 2, P], F32, name="tr", tag="bank")
             tr_tiles[(b, s)] = tr
             for e in range(2):
                 words = a_raw[b][:, 2 * s + e, :].bitcast(F32)
@@ -120,11 +129,12 @@ def tile_gatedgraphconvolution_pa_kernel(tc, adjacent, annotations, gc_bias, ker
         def a_cp(b, s, eng):
             tr = tr_tiles[(b, s)]
             dst = a_grp[b][:, 2 * s * P : (2 * s + 2) * P, :].rearrange("p n t -> p (n t)").bitcast(F32)
-            copy_on(
-                eng,
-                dst.rearrange("p (e r u) -> p e r u", e=2, u=2),
-                tr[:].rearrange("p e u r -> p e r u"),
-            )
+            d = dst.rearrange("p (e r u) -> p e r u", e=2, u=2)
+            s_ = tr[:].rearrange("p e u r -> p e r u")
+            if eng == "v":
+                nc.vector.tensor_copy(out=d, in_=s_)
+            else:
+                nc.scalar.copy(out=d, in_=s_)
 
         def a_q(b):
             nc.vector.quantize_mx(
@@ -134,136 +144,154 @@ def tile_gatedgraphconvolution_pa_kernel(tc, adjacent, annotations, gc_bias, ker
             )
 
         s1_tiles = {}
+        vrows = {}
+        vt_tiles = {}
 
-        def s1_mm(r, g):
+        def s1_mm(r):
             b, it = r // NIT, r % NIT
-            s1 = ps_s1.tile([P, 4, P], BANK_DT, name="s1")
-            s1_tiles[(r, g)] = s1
+            s1 = psum.tile([P, C], BF16, name="s1", tag="bank")
+            s1_tiles[r] = s1
             rows = slice(it * P, (it + 1) * P)
-            for t in range(4):
-                cols = slice(g * 512 + t * P, g * 512 + (t + 1) * P)
-                nc.tensor.matmul_mx(
-                    out=s1[:, t, :],
-                    lhsT=x_cod[b][:, cols].bitcast(FP8X4),
-                    lhsT_scale=x_scl[b][:, cols],
-                    rhs=a_cod[b][:, rows].bitcast(FP8X4),
-                    rhs_scale=a_scl[b][:, rows],
-                    start=True,
-                    stop=True,
-                )
-
-        def s1_out(r, g):
-            nc.vector.tensor_tensor(
-                out=v_grp[r][:, g, :, :],
-                in0=s1_tiles[(r, g)][:].rearrange("p t n -> p n t"),
-                in1=gcb[:, g, :].unsqueeze(1).to_broadcast([P, P, 4]),
-                op=ADD,
+            nc.tensor.matmul_mx(
+                out=s1[:],
+                lhsT=a_cod[b][:, rows].bitcast(FP8X4),
+                lhsT_scale=a_scl[b][:, rows],
+                rhs=x_cod[b][:].bitcast(FP8X4),
+                rhs_scale=x_scl[b][:],
+                start=True,
+                stop=True,
             )
 
-        def v_q(r):
+        def s1_out(r):
+            vrow = vrp.tile([P, C], BF16, name="vrow")
+            vrows[r] = vrow
+            nc.vector.tensor_tensor(out=vrow[:], in0=s1_tiles[r][:], in1=gcbb[:], op=ADD)
+
+        def v_tr(r):
+            vt = psum.tile([P, 2, 2, P], F32, name="vt", tag="bank")
+            vt_tiles[r] = vt
+            words = vrows[r][:].bitcast(F32)
+            for g in range(NG2):
+                for u in range(2):
+                    nc.tensor.transpose(vt[:, g, u, :], words[:, 256 * g + u : 256 * (g + 1) : 2], ident[:])
+
+        def v_cp(r, eng):
+            dst = v_grp[r // VQ][:, r % VQ, :, :, :].rearrange("p g n t -> p (g n t)").bitcast(F32)
+            d = dst.rearrange("p (g n u) -> p g n u", g=NG2, u=2)
+            s_ = vt_tiles[r][:].rearrange("p g u n -> p g n u")
+            if eng == "v":
+                nc.vector.tensor_copy(out=d, in_=s_)
+            else:
+                nc.scalar.copy(out=d, in_=s_)
+
+        def v_q(q):
             nc.vector.quantize_mx(
-                out=v_cod[r][:].rearrange("p g n -> p (g n)").bitcast(FP8X4),
-                scales=v_scl[r][:].rearrange("p g n -> p (g n)"),
-                in_=v_grp[r][:].rearrange("p g n t -> p (g n t)"),
+                out=v_cod[q][:].rearrange("p r g n -> p (r g n)").bitcast(FP8X4),
+                scales=v_scl[q][:].rearrange("p r g n -> p (r g n)"),
+                in_=v_grp[q][:].rearrange("p r g n t -> p (r g n t)"),
             )
 
         kg_tiles = {}
 
-        def k_il(cw, h, g, eng):
-            kg = kgp.tile([P, 512, 4], BF16, name="kg", align_bytes=64)
-            kg_tiles[(cw, h, g)] = kg
-            copy_on(
-                eng,
-                kg[:].rearrange("p (c i) j -> p c j i", i=4),
-                k_raw[cw][g][:, :, h * 512 : (h + 1) * 512].rearrange("p j (c i) -> p c j i", i=4),
-            )
+        def k_il(c, g, lo, hi, eng):
+            if c not in kg_tiles:
+                kg = kgp.tile([P, NG2, 512, 4], BF16, name="kg", align_bytes=64)
+                kg_tiles[c] = kg
+            cw, h = c // NH, c % NH
+            il_on(eng, kg_tiles[c][:, g, lo:hi, :], k_raw[cw][g][:, :, h * 512 + lo : h * 512 + hi])
 
-        def k_q(cw, h, g):
-            cols = slice(h * 512, (h + 1) * 512)
+        def k_q(c):
             nc.vector.quantize_mx(
-                out=k_cod[cw][:, g, cols].bitcast(FP8X4),
-                scales=k_scl[cw][:, g, cols],
-                in_=kg_tiles[(cw, h, g)][:].rearrange("p w j -> p (w j)"),
+                out=k_cod[c][:].rearrange("p g w -> p (g w)").bitcast(FP8X4),
+                scales=k_scl[c][:].rearrange("p g w -> p (g w)"),
+                in_=kg_tiles[c][:].rearrange("p g w j -> p (g w j)"),
             )
 
         s2_tiles = {}
 
-        def s2_mm(cw, r):
-            for h in range(NH):
-                acc = ps_s2.tile([P, 512], F32, name="acc")
-                s2_tiles[(cw, r, h)] = acc
-                cols = slice(h * 512, (h + 1) * 512)
-                for g in range(NG2):
-                    nc.tensor.matmul_mx(
-                        out=acc[:],
-                        lhsT=v_cod[r][:, g, :].bitcast(FP8X4),
-                        lhsT_scale=v_scl[r][:, g, :],
-                        rhs=k_cod[cw][:, g, cols].bitcast(FP8X4),
-                        rhs_scale=k_scl[cw][:, g, cols],
-                        start=(g == 0),
-                        stop=(g == NG2 - 1),
-                    )
-
-        def s2_out(cw, r):
-            b, it = r // NIT, r % NIT
-            o = osb.tile([P, CW], F32, name="o")
-            for h in range(NH):
-                nc.vector.tensor_tensor(
-                    out=o[:, h * 512 : (h + 1) * 512],
-                    in0=s2_tiles[(cw, r, h)][:],
-                    in1=bx[:, cw * CW + h * 512 : cw * CW + (h + 1) * 512],
-                    op=ADD,
+        def s2_mm(c, r):
+            acc = psum.tile([P, 512], F32, name="acc", tag="bank")
+            s2_tiles[(c, r)] = acc
+            for g in range(NG2):
+                nc.tensor.matmul_mx(
+                    out=acc[:],
+                    lhsT=v_cod[r // VQ][:, r % VQ, g, :].bitcast(FP8X4),
+                    lhsT_scale=v_scl[r // VQ][:, r % VQ, g, :],
+                    rhs=k_cod[c][:, g, :].bitcast(FP8X4),
+                    rhs_scale=k_scl[c][:, g, :],
+                    start=(g == 0),
+                    stop=(g == NG2 - 1),
                 )
-            nc.sync.dma_start(out=out_v[b, it, :, cw * CW : (cw + 1) * CW], in_=o[:])
 
+        def s2_out(c, r):
+            b, it = r // NIT, r % NIT
+            o = osb.tile([P, 512], F32, name="o")
+            nc.vector.tensor_tensor(out=o[:], in0=s2_tiles[(c, r)][:], in1=bx[:, c * 512 : (c + 1) * 512], op=ADD)
+            nc.sync.dma_start(out=out_v[b, it, :, c * 512 : (c + 1) * 512], in_=o[:])
 
-        pieces = [(cw, h, g) for cw in range(NCW) for h in range(NH) for g in range(NG2)]
-        units1 = [(r, g) for r in range(NRT) for g in range(NG2)]
-        units2 = [(cw, r) for cw in range(NCW) for r in range(NRT)]
-        KGB = 4
-
-        def k_q_then_il(j):
-            k_q(*pieces[j])
-            if j + KGB < len(pieces):
-                k_il(*pieces[j + KGB], "s")
-
-        x_il(0, 0, "v")
-        x_il(0, 1, "s")
+        x_il(0, 0, 256, "v")
+        x_il(0, 256, 512, "v")
+        x_q(0, 0, 512)
+        x_il(0, 768, 1024, "s")
+        x_il(0, 512, 768, "v")
         a_tr(0, 0)
         a_tr(0, 1)
-        x_q(0, 0)
-        a_cp(0, 0, "v")
-        a_cp(0, 1, "v")
+        a_cp(0, 0, "s")
+        a_cp(0, 1, "s")
+        x_q(0, 512, 1024)
+        a_q(0)
+        for r in range(4):
+            s1_mm(r)
+        x_il(1, 0, 512, "v")
+        x_il(1, 512, 1024, "s")
         a_tr(1, 0)
         a_tr(1, 1)
         a_cp(1, 0, "s")
         a_cp(1, 1, "s")
-        x_q(0, 1)
-        a_q(0)
+        s1_out(0)
+        s1_out(1)
+        v_tr(0)
+        v_tr(1)
+        x_q(1, 0, 1024)
+        s1_out(2)
+        s1_out(3)
         a_q(1)
-        x_il(1, 0, "v")
-        x_il(1, 1, "s")
-        for j in range(KGB):
-            k_il(*pieces[j], "s")
+        v_tr(2)
+        v_tr(3)
+        for r in range(4, 8):
+            s1_mm(r)
+        k_il(0, 0, 0, 512, "s")
+        k_il(0, 1, 0, 512, "v")
+        for r in range(4):
+            v_cp(r, "s")
+        for r in range(4, 8):
+            s1_out(r)
+            v_tr(r)
+            if r == 5:
+                v_q(0)
+        v_q(1)
+        k_q(0)
+        for r in range(4, 8):
+            v_cp(r, "s")
+        v_q(2)
+        v_q(3)
+        k_il(1, 0, 0, 512, "s")
+        k_il(1, 1, 0, 512, "s")
 
-        extra1 = {1: lambda: x_q(1, 0), 4: lambda: x_q(1, 1), 8: lambda: k_q_then_il(0), 10: lambda: k_q_then_il(1), 12: lambda: k_q_then_il(2), 14: lambda: k_q_then_il(3)}
-        s1_mm(*units1[0])
-        for i in range(len(units1)):
-            r, g = units1[i]
-            if i in extra1:
-                extra1[i]()
-            if i + 1 < len(units1):
-                s1_mm(*units1[i + 1])
-            s1_out(r, g)
-            if g == 1 and r >= 1:
-                v_q(r - 1)
-        v_q(NRT - 1)
-
-        s2_mm(*units2[0])
-        for i in range(len(units2)):
-            cw, r = units2[i]
-            if i + 1 < len(units2):
-                s2_mm(*units2[i + 1])
-            s2_out(cw, r)
-            if cw + 1 < NCW and r % 2 == 0:
-                k_q_then_il(4 * (cw + 1) + r // 2)
+        banks = [(c, r) for c in range(NCH) for r in range(NRT)]
+        AHEAD = 3
+        QPOS = 5
+        for i in range(AHEAD):
+            s2_mm(banks[i][0], banks[i][1])
+        k_il(2, 0, 0, 512, "s")
+        k_il(2, 1, 0, 512, "s")
+        for i in range(len(banks)):
+            c, r = banks[i]
+            if r == QPOS and c + 1 < NCH:
+                k_q(c + 1)
+                if c + 3 < NCH:
+                    k_il(c + 3, 0, 0, 512, "s")
+                    k_il(c + 3, 1, 0, 512, "g")
+            if i + AHEAD < len(banks):
+                s2_mm(banks[i + AHEAD][0], banks[i + AHEAD][1])
+            s2_out(c, r)

@@ -46,6 +46,8 @@ def tile_gatedgraphconvolution_pa_kernel(tc, adjacent, annotations, gc_bias, ker
         x_raw = [keep.tile([P, 4, C], BF16, name="x_raw%d" % b) for b in range(B)]
         a_raw = [keep.tile([P, NIT, N], BF16, name="a_raw%d" % b) for b in range(B)]
         k_raw = [[keep.tile([P, 4, CW], BF16, name="k_raw%d_%d" % (cw, g)) for g in range(NG2)] for cw in range(NCW)]
+        ones = keep.tile([P, P], BF16, name="ones")
+        b_row = keep.tile([P, C], BF16, name="b_row")
         gcbb = keep.tile([P, C], BF16, name="gcbb")
         bx = keep.tile([P, G], BF16, name="bx")
 
@@ -79,12 +81,14 @@ def tile_gatedgraphconvolution_pa_kernel(tc, adjacent, annotations, gc_bias, ker
                 in_=k_v[g, :, :, cw * CW + h * 512 : cw * CW + (h + 1) * 512],
             )
 
+        nc.vector.memset(ones[:], 1.0)
+        nc.vector.memset(b_row[:], 0.0)
+        nc.scalar.dma_start(out=b_row[0:1, :], in_=gc_bias[0])
         load_x(0, 0, 256)
         load_x(0, 256, 512)
         load_x(0, 512, 1024)
         load_a(0)
         load_x(1, 0, 1024)
-        nc.sync.dma_start(out=gcbb[:], in_=gc_bias[0, 0, :].partition_broadcast(P))
         load_a(1)
         for h in range(NH):
             for g in range(NG2):
@@ -115,6 +119,18 @@ def tile_gatedgraphconvolution_pa_kernel(tc, adjacent, annotations, gc_bias, ker
                 scales=x_scl[b][:, lo:hi],
                 in_=x_grp[b][:, lo:hi, :].rearrange("p c j -> p (c j)"),
             )
+
+        def spread_gc_bias():
+            pb = psum.tile([P, C], BF16, name="pb", tag="bank")
+            for hh in range(2):
+                nc.tensor.matmul(
+                    out=pb[:, hh * 512 : (hh + 1) * 512],
+                    lhsT=ones[:],
+                    rhs=b_row[:, hh * 512 : (hh + 1) * 512],
+                    start=True,
+                    stop=True,
+                )
+            nc.scalar.copy(out=gcbb[:], in_=pb[:])
 
         tr_tiles = {}
 
@@ -238,6 +254,7 @@ def tile_gatedgraphconvolution_pa_kernel(tc, adjacent, annotations, gc_bias, ker
         a_tr(0, 1)
         a_cp(0, 0, "s")
         a_cp(0, 1, "s")
+        spread_gc_bias()
         x_q(0, 512, 1024)
         a_q(0)
         for r in range(4):

@@ -22,16 +22,17 @@ CW = 1024
 NCW = G // CW
 NH = CW // 512
 NCH = G // 512
-VQ = 2
+VQ = 4
 
 
 def tile_gatedgraphconvolution_pa_kernel(tc, adjacent, annotations, gc_bias, kernel, bias_x, out):
     nc = tc.nc
     with ExitStack() as ctx:
         keep = ctx.enter_context(tc.tile_pool(name="keep", bufs=1))
-        kgp = ctx.enter_context(tc.tile_pool(name="kgp", bufs=2))
+        chain = ctx.enter_context(tc.tile_pool(name="chain", bufs=1))
         vrp = ctx.enter_context(tc.tile_pool(name="vrp", bufs=4))
         osb = ctx.enter_context(tc.tile_pool(name="osb", bufs=8))
+        sidep = ctx.enter_context(tc.tile_pool(name="sidep", bufs=2))
         psum = ctx.enter_context(tc.psum_pool(name="psum", bufs=8))
         ctx.enter_context(tc.manual_schedule())
 
@@ -57,7 +58,10 @@ def tile_gatedgraphconvolution_pa_kernel(tc, adjacent, annotations, gc_bias, ker
         a_grp = [keep.tile([P, N, 4], BF16, name="a_grp%d" % b, align_bytes=64) for b in range(B)]
         a_cod = [keep.tile([P, N], U32, name="a_cod%d" % b, align_bytes=64) for b in range(B)]
         a_scl = [keep.tile([P, N], U8, name="a_scl%d" % b, align_bytes=64) for b in range(B)]
-        v_grp = [keep.tile([P, VQ, NG2, P, 4], BF16, name="v_grp%d" % q, align_bytes=64) for q in range(NRT // VQ)]
+        v_grp = [
+            keep.tile([P, VQ, NG2, P, 4], BF16, name="v_grp0", align_bytes=64),
+            chain.tile([P, VQ, NG2, P, 4], BF16, name="v_grp1", tag="link", align_bytes=64),
+        ]
         v_cod = [keep.tile([P, VQ, NG2, P], U32, name="v_cod%d" % q, align_bytes=64) for q in range(NRT // VQ)]
         v_scl = [keep.tile([P, VQ, NG2, P], U8, name="v_scl%d" % q, align_bytes=64) for q in range(NRT // VQ)]
         k_cod = [keep.tile([P, NG2, 512], U32, name="k_cod%d" % c, align_bytes=64) for c in range(NCH)]
@@ -211,7 +215,10 @@ def tile_gatedgraphconvolution_pa_kernel(tc, adjacent, annotations, gc_bias, ker
 
         def k_il(c, g, lo, hi, eng):
             if c not in kg_tiles:
-                kg = kgp.tile([P, NG2, 512, 4], BF16, name="kg", align_bytes=64)
+                if c == 0:
+                    kg = keep.tile([P, NG2, 512, 4], BF16, name="kg0", align_bytes=64)
+                else:
+                    kg = chain.tile([P, NG2, 512, 4], BF16, name="kg", tag="link", align_bytes=64)
                 kg_tiles[c] = kg
             cw, h = c // NH, c % NH
             il_on(eng, kg_tiles[c][:, g, lo:hi, :], k_raw[cw][g][:, :, h * 512 + lo : h * 512 + hi])
@@ -239,11 +246,23 @@ def tile_gatedgraphconvolution_pa_kernel(tc, adjacent, annotations, gc_bias, ker
                     stop=(g == NG2 - 1),
                 )
 
-        def s2_out(c, r):
+        def store(c, r, o):
             b, it = r // NIT, r % NIT
+            nc.sync.dma_start(out=out_v[b, it, :, c * 512 : (c + 1) * 512], in_=o[:])
+
+        def s2_out(c, r):
             o = osb.tile([P, 512], F32, name="o")
             nc.vector.tensor_tensor(out=o[:], in0=s2_tiles[(c, r)][:], in1=bx[:, c * 512 : (c + 1) * 512], op=ADD)
-            nc.sync.dma_start(out=out_v[b, it, :, c * 512 : (c + 1) * 512], in_=o[:])
+            store(c, r, o)
+
+        side_tiles = {}
+
+        def s2_side(c, r):
+            sums = sidep.tile([P, 512], F32, name="sums")
+            nc.scalar.copy(out=sums[:], in_=s2_tiles[(c, r)][:])
+            so = sidep.tile([P, 512], F32, name="so")
+            side_tiles[(c, r)] = so
+            nc.gpsimd.tensor_tensor(out=so[:], in0=sums[:], in1=bx[:, c * 512 : (c + 1) * 512], op=ADD)
 
         x_il(0, 0, 256, "v")
         x_il(0, 256, 512, "v")
@@ -284,31 +303,36 @@ def tile_gatedgraphconvolution_pa_kernel(tc, adjacent, annotations, gc_bias, ker
         for r in range(4, 8):
             s1_out(r)
             v_tr(r)
-            if r == 5:
-                v_q(0)
-        v_q(1)
+        v_q(0)
         k_q(0)
         for r in range(4, 8):
             v_cp(r, "s")
-        v_q(2)
-        v_q(3)
-        k_il(1, 0, 0, 512, "s")
-        k_il(1, 1, 0, 512, "s")
 
         banks = [(c, r) for c in range(NCH) for r in range(NRT)]
         AHEAD = 3
         QPOS = 5
         for i in range(AHEAD):
             s2_mm(banks[i][0], banks[i][1])
-        k_il(2, 0, 0, 512, "s")
-        k_il(2, 1, 0, 512, "s")
+        GW = 416
+
+        v_q(1)
+        k_il(1, 1, 0, 512 - GW, "s")
+        k_il(1, 1, 512 - GW, 512, "g")
+        k_il(1, 0, 0, 512, "s")
         for i in range(len(banks)):
             c, r = banks[i]
+            if r == QPOS and c >= 1:
+                store(c, 0, side_tiles[(c, 0)])
             if r == QPOS and c + 1 < NCH:
                 k_q(c + 1)
-                if c + 3 < NCH:
-                    k_il(c + 3, 0, 0, 512, "s")
-                    k_il(c + 3, 1, 0, 512, "g")
+                if c + 2 < NCH:
+                    k_il(c + 2, 1, 0, 512 - GW, "s")
+                    k_il(c + 2, 1, 512 - GW, 512, "g")
             if i + AHEAD < len(banks):
                 s2_mm(banks[i + AHEAD][0], banks[i + AHEAD][1])
-            s2_out(c, r)
+            if r == 0 and c >= 1:
+                s2_side(c, r)
+                if c + 1 < NCH:
+                    k_il(c + 1, 0, 0, 512, "s")
+            else:
+                s2_out(c, r)

@@ -48,7 +48,7 @@ def tile_gatedgraphconvolution_pa_kernel(tc, adjacent, annotations, gc_bias, ker
         a_raw = [keep.tile([P, NIT, N], BF16, name="a_raw%d" % b) for b in range(B)]
         k_raw = [[keep.tile([P, 4, CW], BF16, name="k_raw%d_%d" % (cw, g)) for g in range(NG2)] for cw in range(NCW)]
         ones = keep.tile([P, P], BF16, name="ones")
-        b_row = keep.tile([P, C], BF16, name="b_row")
+        b_row = keep.tile([P, C + G], BF16, name="b_row")
         gcbb = keep.tile([P, C], BF16, name="gcbb")
         bx = keep.tile([P, G], BF16, name="bx")
 
@@ -87,7 +87,8 @@ def tile_gatedgraphconvolution_pa_kernel(tc, adjacent, annotations, gc_bias, ker
 
         nc.vector.memset(ones[:], 1.0)
         nc.vector.memset(b_row[:], 0.0)
-        nc.scalar.dma_start(out=b_row[0:1, :], in_=gc_bias[0])
+        nc.scalar.dma_start(out=b_row[0:1, 0:C], in_=gc_bias[0])
+        nc.scalar.dma_start(out=b_row[0:1, C : C + G], in_=bias_x.rearrange("(o g) -> o g", o=1))
         load_x(0, 0, 256)
         load_x(0, 256, 512)
         load_x(0, 512, 1024)
@@ -97,7 +98,6 @@ def tile_gatedgraphconvolution_pa_kernel(tc, adjacent, annotations, gc_bias, ker
         for h in range(NH):
             for g in range(NG2):
                 load_k_half(0, g, h)
-        nc.sync.dma_start(out=bx[:], in_=bias_x.partition_broadcast(P))
         for cw in range(1, NCW):
             for g in range(NG2):
                 load_k(cw, g)
@@ -124,17 +124,17 @@ def tile_gatedgraphconvolution_pa_kernel(tc, adjacent, annotations, gc_bias, ker
                 in_=x_grp[b][:, lo:hi, :].rearrange("p c j -> p (c j)"),
             )
 
-        def spread_gc_bias():
-            pb = psum.tile([P, C], BF16, name="pb", tag="bank")
+        def spread(dst, lo):
+            pb = psum.tile([P, 1024], BF16, name="pb", tag="bank")
             for hh in range(2):
                 nc.tensor.matmul(
                     out=pb[:, hh * 512 : (hh + 1) * 512],
                     lhsT=ones[:],
-                    rhs=b_row[:, hh * 512 : (hh + 1) * 512],
+                    rhs=b_row[:, lo + hh * 512 : lo + (hh + 1) * 512],
                     start=True,
                     stop=True,
                 )
-            nc.scalar.copy(out=gcbb[:], in_=pb[:])
+            nc.scalar.copy(out=dst, in_=pb[:])
 
         tr_tiles = {}
 
@@ -273,7 +273,7 @@ def tile_gatedgraphconvolution_pa_kernel(tc, adjacent, annotations, gc_bias, ker
         a_tr(0, 1)
         a_cp(0, 0, "s")
         a_cp(0, 1, "s")
-        spread_gc_bias()
+        spread(gcbb[:], 0)
         x_q(0, 512, 1024)
         a_q(0)
         for r in range(4):
@@ -307,6 +307,8 @@ def tile_gatedgraphconvolution_pa_kernel(tc, adjacent, annotations, gc_bias, ker
         k_q(0)
         for r in range(4, 8):
             v_cp(r, "s")
+        for cw in range(NCW):
+            spread(bx[:, cw * CW : (cw + 1) * CW], C + cw * CW)
 
         banks = [(c, r) for c in range(NCH) for r in range(NRT)]
         AHEAD = 3

@@ -30,6 +30,7 @@ def tile_gatedgraphconvolution_pa_kernel(tc, adjacent, annotations, gc_bias, ker
     with ExitStack() as ctx:
         keep = ctx.enter_context(tc.tile_pool(name="keep", bufs=1))
         chain = ctx.enter_context(tc.tile_pool(name="chain", bufs=1))
+        kgp = ctx.enter_context(tc.tile_pool(name="kgp", bufs=2))
         vrp = ctx.enter_context(tc.tile_pool(name="vrp", bufs=4))
         osb = ctx.enter_context(tc.tile_pool(name="osb", bufs=8))
         sidep = ctx.enter_context(tc.tile_pool(name="sidep", bufs=2))
@@ -214,20 +215,20 @@ def tile_gatedgraphconvolution_pa_kernel(tc, adjacent, annotations, gc_bias, ker
         kg_tiles = {}
 
         def k_il(c, g, lo, hi, eng):
-            if c not in kg_tiles:
-                if c == 0:
-                    kg = keep.tile([P, NG2, 512, 4], BF16, name="kg0", align_bytes=64)
+            if (c, g) not in kg_tiles:
+                if g == 0 or c == 0:
+                    kg = kgp.tile([P, 512, 4], BF16, name="kg", align_bytes=64)
                 else:
-                    kg = chain.tile([P, NG2, 512, 4], BF16, name="kg", tag="link", align_bytes=64)
-                kg_tiles[c] = kg
+                    kg = chain.tile([P, 512, 4], BF16, name="kl", tag="link", align_bytes=64)
+                kg_tiles[(c, g)] = kg
             cw, h = c // NH, c % NH
-            il_on(eng, kg_tiles[c][:, g, lo:hi, :], k_raw[cw][g][:, :, h * 512 + lo : h * 512 + hi])
+            il_on(eng, kg_tiles[(c, g)][:, lo:hi, :], k_raw[cw][g][:, :, h * 512 + lo : h * 512 + hi])
 
-        def k_q(c):
+        def k_q(c, g):
             nc.vector.quantize_mx(
-                out=k_cod[c][:].rearrange("p g w -> p (g w)").bitcast(FP8X4),
-                scales=k_scl[c][:].rearrange("p g w -> p (g w)"),
-                in_=kg_tiles[c][:].rearrange("p g w j -> p (g w j)"),
+                out=k_cod[c][:, g, :].bitcast(FP8X4),
+                scales=k_scl[c][:, g, :],
+                in_=kg_tiles[(c, g)][:].rearrange("p w j -> p (w j)"),
             )
 
         s2_tiles = {}
@@ -304,37 +305,42 @@ def tile_gatedgraphconvolution_pa_kernel(tc, adjacent, annotations, gc_bias, ker
             s1_out(r)
             v_tr(r)
         v_q(0)
-        k_q(0)
+        k_q(0, 0)
+        k_q(0, 1)
         for r in range(4, 8):
             v_cp(r, "s")
-        for cw in range(NCW):
-            spread(bx[:, cw * CW : (cw + 1) * CW], C + cw * CW)
+        spread(bx[:, 0:CW], C)
+        k_il(1, 0, 0, 512, "s")
 
         banks = [(c, r) for c in range(NCH) for r in range(NRT)]
         AHEAD = 3
         QPOS = 5
         for i in range(AHEAD):
             s2_mm(banks[i][0], banks[i][1])
-        GW = 416
+        GW = 256
 
         v_q(1)
-        k_il(1, 1, 0, 512 - GW, "s")
         k_il(1, 1, 512 - GW, 512, "g")
-        k_il(1, 0, 0, 512, "s")
+        k_il(1, 1, 0, 512 - GW, "s")
+        k_il(2, 0, 0, 512, "s")
         for i in range(len(banks)):
             c, r = banks[i]
             if r == QPOS and c >= 1:
                 store(c, 0, side_tiles[(c, 0)])
             if r == QPOS and c + 1 < NCH:
-                k_q(c + 1)
+                k_q(c + 1, 0)
+                k_q(c + 1, 1)
                 if c + 2 < NCH:
-                    k_il(c + 2, 1, 0, 512 - GW, "s")
                     k_il(c + 2, 1, 512 - GW, 512, "g")
             if i + AHEAD < len(banks):
                 s2_mm(banks[i + AHEAD][0], banks[i + AHEAD][1])
             if r == 0 and c >= 1:
                 s2_side(c, r)
                 if c + 1 < NCH:
-                    k_il(c + 1, 0, 0, 512, "s")
+                    k_il(c + 1, 1, 0, 512 - GW, "s")
+                if c + 2 < NCH:
+                    k_il(c + 2, 0, 0, 512, "s")
+                if c % NH == 1 and c + 1 < NCH:
+                    spread(bx[:, (c + 1) * 512 : (c + 1) * 512 + CW], C + (c + 1) * 512)
             else:
                 s2_out(c, r)

@@ -49,7 +49,7 @@ def tile_gatedgraphconvolution_pa_kernel(tc, adjacent, annotations, gc_bias, ker
         a_raw = [keep.tile([P, NIT, N], BF16, name="a_raw%d" % b) for b in range(B)]
         k_raw = [[keep.tile([P, 4, CW], BF16, name="k_raw%d_%d" % (cw, g)) for g in range(NG2)] for cw in range(NCW)]
         ones = keep.tile([P, P], BF16, name="ones")
-        b_row = keep.tile([P, C + G], BF16, name="b_row")
+        b_row = keep.tile([P, C + CW], BF16, name="b_row")
         gcbb = keep.tile([P, C], BF16, name="gcbb")
         bx = keep.tile([P, G], BF16, name="bx")
 
@@ -89,9 +89,8 @@ def tile_gatedgraphconvolution_pa_kernel(tc, adjacent, annotations, gc_bias, ker
         nc.vector.memset(ones[:], 1.0)
         nc.vector.memset(b_row[:], 0.0)
         nc.scalar.dma_start(out=b_row[0:1, 0:C], in_=gc_bias[0])
-        nc.scalar.dma_start(out=b_row[0:1, C : C + G], in_=bias_x.rearrange("(o g) -> o g", o=1))
-        load_x(0, 0, 256)
-        load_x(0, 256, 512)
+        nc.scalar.dma_start(out=b_row[0:1, C : C + CW], in_=bias_x.rearrange("(o g) -> o g", o=1)[:, 0:CW])
+        load_x(0, 0, 512)
         load_x(0, 512, 1024)
         load_a(0)
         load_x(1, 0, 1024)
@@ -102,6 +101,7 @@ def tile_gatedgraphconvolution_pa_kernel(tc, adjacent, annotations, gc_bias, ker
         for cw in range(1, NCW):
             for g in range(NG2):
                 load_k(cw, g)
+        nc.sync.dma_start(out=bx[:, CW:G], in_=bias_x[CW:G].partition_broadcast(P))
 
         def il_on(eng, dst, src):
             if eng == "v":
@@ -115,8 +115,13 @@ def tile_gatedgraphconvolution_pa_kernel(tc, adjacent, annotations, gc_bias, ker
                     out=dst, in0=src.rearrange("p j w -> p w j"), scalar1=1.0, scalar2=0.0, op0=MULT, op1=ADD
                 )
 
-        def x_il(b, lo, hi, eng):
-            il_on(eng, x_grp[b][:, lo:hi, :], x_raw[b][:, :, lo:hi])
+        def x_il(b, g, u, eng):
+            dst = x_grp[b][:, (2 * g + u) * 256 : (2 * g + u + 1) * 256, :].rearrange("p (q e) j -> p q e j", e=2)
+            src = x_raw[b][:, :, g * 512 : (g + 1) * 512].rearrange("p j (q u e) -> p u q e j", u=2, e=2)[:, u, :, :, :]
+            if eng == "v":
+                nc.vector.tensor_copy(out=dst, in_=src)
+            else:
+                nc.scalar.copy(out=dst, in_=src)
 
         def x_q(b, lo, hi):
             nc.vector.quantize_mx(
@@ -125,7 +130,7 @@ def tile_gatedgraphconvolution_pa_kernel(tc, adjacent, annotations, gc_bias, ker
                 in_=x_grp[b][:, lo:hi, :].rearrange("p c j -> p (c j)"),
             )
 
-        def spread(dst, lo):
+        def spread(dst, lo, turn=False):
             pb = psum.tile([P, 1024], BF16, name="pb", tag="bank")
             for hh in range(2):
                 nc.tensor.matmul(
@@ -135,7 +140,13 @@ def tile_gatedgraphconvolution_pa_kernel(tc, adjacent, annotations, gc_bias, ker
                     start=True,
                     stop=True,
                 )
-            nc.scalar.copy(out=dst, in_=pb[:])
+            if turn:
+                nc.scalar.copy(
+                    out=dst.bitcast(F32).rearrange("p (g u q) -> p g u q", g=NG2, u=2),
+                    in_=pb[:].bitcast(F32).rearrange("p (g q u) -> p g u q", g=NG2, u=2),
+                )
+            else:
+                nc.scalar.copy(out=dst, in_=pb[:])
 
         tr_tiles = {}
 
@@ -194,7 +205,7 @@ def tile_gatedgraphconvolution_pa_kernel(tc, adjacent, annotations, gc_bias, ker
             words = vrows[r][:].bitcast(F32)
             for g in range(NG2):
                 for u in range(2):
-                    nc.tensor.transpose(vt[:, g, u, :], words[:, 256 * g + u : 256 * (g + 1) : 2], ident[:])
+                    nc.tensor.transpose(vt[:, g, u, :], words[:, (2 * g + u) * P : (2 * g + u + 1) * P], ident[:])
 
         def v_cp(r, eng):
             dst = v_grp[r // VQ][:, r % VQ, :, :, :].rearrange("p g n t -> p (g n t)").bitcast(F32)
@@ -265,22 +276,24 @@ def tile_gatedgraphconvolution_pa_kernel(tc, adjacent, annotations, gc_bias, ker
             side_tiles[(c, r)] = so
             nc.gpsimd.tensor_tensor(out=so[:], in0=sums[:], in1=bx[:, c * 512 : (c + 1) * 512], op=ADD)
 
-        x_il(0, 0, 256, "v")
-        x_il(0, 256, 512, "v")
+        x_il(0, 0, 0, "v")
+        x_il(0, 0, 1, "v")
         x_q(0, 0, 512)
-        x_il(0, 768, 1024, "s")
-        x_il(0, 512, 768, "v")
+        x_il(0, 1, 1, "s")
+        x_il(0, 1, 0, "v")
         a_tr(0, 0)
         a_tr(0, 1)
         a_cp(0, 0, "s")
         a_cp(0, 1, "s")
-        spread(gcbb[:], 0)
+        spread(gcbb[:], 0, turn=True)
         x_q(0, 512, 1024)
         a_q(0)
         for r in range(4):
             s1_mm(r)
-        x_il(1, 0, 512, "v")
-        x_il(1, 512, 1024, "s")
+        x_il(1, 0, 0, "v")
+        x_il(1, 0, 1, "v")
+        x_il(1, 1, 0, "s")
+        x_il(1, 1, 1, "s")
         a_tr(1, 0)
         a_tr(1, 1)
         a_cp(1, 0, "s")
@@ -340,7 +353,5 @@ def tile_gatedgraphconvolution_pa_kernel(tc, adjacent, annotations, gc_bias, ker
                     k_il(c + 1, 1, 0, 512 - GW, "s")
                 if c + 2 < NCH:
                     k_il(c + 2, 0, 0, 512, "s")
-                if c % NH == 1 and c + 1 < NCH:
-                    spread(bx[:, (c + 1) * 512 : (c + 1) * 512 + CW], C + (c + 1) * 512)
             else:
                 s2_out(c, r)

@@ -32,7 +32,7 @@ def tile_gatedgraphconvolution_pa_kernel(tc, adjacent, annotations, gc_bias, ker
         chain = ctx.enter_context(tc.tile_pool(name="chain", bufs=1))
         kgp = ctx.enter_context(tc.tile_pool(name="kgp", bufs=2))
         vrp = ctx.enter_context(tc.tile_pool(name="vrp", bufs=4))
-        osb = ctx.enter_context(tc.tile_pool(name="osb", bufs=8))
+        osb = ctx.enter_context(tc.tile_pool(name="osb", bufs=6))
         sidep = ctx.enter_context(tc.tile_pool(name="sidep", bufs=2))
         psum = ctx.enter_context(tc.psum_pool(name="psum", bufs=8))
         ctx.enter_context(tc.manual_schedule())
@@ -68,7 +68,7 @@ def tile_gatedgraphconvolution_pa_kernel(tc, adjacent, annotations, gc_bias, ker
         k_cod = [keep.tile([P, NG2, 512], U32, name="k_cod%d" % c, align_bytes=64) for c in range(NCH)]
         k_scl = [keep.tile([P, NG2, 512], U8, name="k_scl%d" % c, align_bytes=64) for c in range(NCH)]
 
-        out_v = out.rearrange("(b m i) g -> b i m g", b=B, i=NIT)
+        out_v = out.rearrange("(b m i) g -> b m i g", b=B, i=NIT)
         k_v = kernel.rearrange("(g p j) w -> g p j w", g=NG2, j=4)
 
         def load_x(b, lo, hi):
@@ -258,23 +258,32 @@ def tile_gatedgraphconvolution_pa_kernel(tc, adjacent, annotations, gc_bias, ker
                     stop=(g == NG2 - 1),
                 )
 
-        def store(c, r, o):
+        o_tiles = {}
+
+        def o_half(c, r):
+            if (c, r // 2) not in o_tiles:
+                o_tiles[(c, r // 2)] = osb.tile([P, 2, 512], F32, name="o")
+            return o_tiles[(c, r // 2)][:, r % 2, :]
+
+        def store2(c, r):
             b, it = r // NIT, r % NIT
-            nc.sync.dma_start(out=out_v[b, it, :, c * 512 : (c + 1) * 512], in_=o[:])
+            nc.sync.dma_start(out=out_v[b, :, it : it + 2, c * 512 : (c + 1) * 512], in_=o_tiles[(c, r // 2)][:])
+
+        def store1(c, r):
+            b, it = r // NIT, r % NIT
+            nc.sync.dma_start(out=out_v[b, :, it, c * 512 : (c + 1) * 512], in_=o_half(c, r))
 
         def s2_out(c, r):
-            o = osb.tile([P, 512], F32, name="o")
-            nc.vector.tensor_tensor(out=o[:], in0=s2_tiles[(c, r)][:], in1=bx[:, c * 512 : (c + 1) * 512], op=ADD)
-            store(c, r, o)
-
-        side_tiles = {}
+            nc.vector.tensor_tensor(out=o_half(c, r), in0=s2_tiles[(c, r)][:], in1=bx[:, c * 512 : (c + 1) * 512], op=ADD)
+            if c == NCH - 1 and r >= NRT - 2:
+                store1(c, r)
+            elif r % 2 == 1 and not (r == 1 and c >= 1):
+                store2(c, r - 1)
 
         def s2_side(c, r):
             sums = sidep.tile([P, 512], F32, name="sums")
             nc.scalar.copy(out=sums[:], in_=s2_tiles[(c, r)][:])
-            so = sidep.tile([P, 512], F32, name="so")
-            side_tiles[(c, r)] = so
-            nc.gpsimd.tensor_tensor(out=so[:], in0=sums[:], in1=bx[:, c * 512 : (c + 1) * 512], op=ADD)
+            nc.gpsimd.tensor_tensor(out=o_half(c, r), in0=sums[:], in1=bx[:, c * 512 : (c + 1) * 512], op=ADD)
 
         x_il(0, 0, 0, "v")
         x_il(0, 0, 1, "v")
@@ -339,7 +348,7 @@ def tile_gatedgraphconvolution_pa_kernel(tc, adjacent, annotations, gc_bias, ker
         for i in range(len(banks)):
             c, r = banks[i]
             if r == QPOS and c >= 1:
-                store(c, 0, side_tiles[(c, 0)])
+                store2(c, 0)
             if r == QPOS and c + 1 < NCH:
                 k_q(c + 1, 0)
                 k_q(c + 1, 1)

from contextlib import ExitStack

import concourse.mybir as mybir
from concourse.masks import make_identity

F32 = mybir.dt.float32
BF16 = mybir.dt.bfloat16
U32 = mybir.dt.uint32
U8 = mybir.dt.uint8
FP8X4 = mybir.dt.float8_e4m3fn_x4
ADD = mybir.AluOpType.add
MULT = mybir.AluOpType.mult

P = 128
B, N, C, G = 2, 512, 1024, 3072
FLOPS = 2 * B * N * N * C + 2 * B * N * C * G

NIT = N // P
NRT = B * NIT
NG2 = C // 512
CW = 1024
NCW = G // CW
NH = CW // 512
NCH = G // 512
VQ = 4


def tile_gatedgraphconvolution_pa_kernel(tc, adjacent, annotations, gc_bias, kernel, bias_x, out):
    nc = tc.nc
    with ExitStack() as ctx:
        keep = ctx.enter_context(tc.tile_pool(name="keep", bufs=1))
        chain = ctx.enter_context(tc.tile_pool(name="chain", bufs=1))
        kgp = ctx.enter_context(tc.tile_pool(name="kgp", bufs=2))
        vrp = ctx.enter_context(tc.tile_pool(name="vrp", bufs=4))
        osb = ctx.enter_context(tc.tile_pool(name="osb", bufs=6))
        sidep = ctx.enter_context(tc.tile_pool(name="sidep", bufs=2))
        psum = ctx.enter_context(tc.psum_pool(name="psum", bufs=8))
        ctx.enter_context(tc.manual_schedule())

        warm_in = keep.tile([P, 8], F32, name="warm_in")
        warm_out = keep.tile([P, 8], F32, name="warm_out")
        nc.vector.memset(warm_in[:], 0.0)
        nc.scalar.copy(out=warm_out[:], in_=warm_in[:])

        ident = keep.tile([P, P], F32, name="ident")
        make_identity(nc, ident[:])

        x_raw = [keep.tile([P, 4, C], BF16, name="x_raw%d" % b) for b in range(B)]
        a_raw = [keep.tile([P, NIT, N], BF16, name="a_raw%d" % b) for b in range(B)]
        k_raw = [[keep.tile([P, 4, CW], BF16, name="k_raw%d_%d" % (cw, g)) for g in range(NG2)] for cw in range(NCW)]
        ones = keep.tile([P, P], BF16, name="ones")
        b_row = keep.tile([P, C + CW], BF16, name="b_row")
        gcbb = keep.tile([P, C], BF16, name="gcbb")
        bx = keep.tile([P, G], BF16, name="bx")

        x_grp = [keep.tile([P, C, 4], BF16, name="x_grp%d" % b, align_bytes=64) for b in range(B)]
        x_cod = [keep.tile([P, C], U32, name="x_cod%d" % b, align_bytes=64) for b in range(B)]
        x_scl = [keep.tile([P, C], U8, name="x_scl%d" % b, align_bytes=64) for b in range(B)]
        a_grp = [keep.tile([P, N, 4], BF16, name="a_grp%d" % b, align_bytes=64) for b in range(B)]
        a_cod = [keep.tile([P, N], U32, name="a_cod%d" % b, align_bytes=64) for b in range(B)]
        a_scl = [keep.tile([P, N], U8, name="a_scl%d" % b, align_bytes=64) for b in range(B)]
        v_grp = [
            keep.tile([P, VQ, NG2, P, 4], BF16, name="v_grp0", align_bytes=64),
            chain.tile([P, VQ, NG2, P, 4], BF16, name="v_grp1", tag="link", align_bytes=64),
        ]
        v_cod = [keep.tile([P, VQ, NG2, P], U32, name="v_cod%d" % q, align_bytes=64) for q in range(NRT // VQ)]
        v_scl = [keep.tile([P, VQ, NG2, P], U8, name="v_scl%d" % q, align_bytes=64) for q in range(NRT // VQ)]
        k_cod = [keep.tile([P, NG2, 512], U32, name="k_cod%d" % c, align_bytes=64) for c in range(NCH)]
        k_scl = [keep.tile([P, NG2, 512], U8, name="k_scl%d" % c, align_bytes=64) for c in range(NCH)]

        out_v = out.rearrange("(b m i) g -> b m i g", b=B, i=NIT)
        k_v = kernel.rearrange("(g p j) w -> g p j w", g=NG2, j=4)

        def load_x(b, lo, hi):
            nc.sync.dma_start(out=x_raw[b][:, :, lo:hi], in_=annotations[b].rearrange("(p j) c -> p j c", j=4)[:, :, lo:hi])

        def load_a(b):
            nc.sync.dma_start(out=a_raw[b][:], in_=adjacent[b].rearrange("(p i) j -> p i j", i=NIT))

        def load_k(cw, g):
            nc.sync.dma_start(out=k_raw[cw][g][:], in_=k_v[g, :, :, cw * CW : (cw + 1) * CW])

        def load_k_half(cw, g, h):
            nc.sync.dma_start(
                out=k_raw[cw][g][:, :, h * 512 : (h + 1) * 512],
                in_=k_v[g, :, :, cw * CW + h * 512 : cw * CW + (h + 1) * 512],
            )

        nc.vector.memset(ones[:], 1.0)
        nc.vector.memset(b_row[:], 0.0)
        nc.scalar.dma_start(out=b_row[0:1, 0:C], in_=gc_bias[0])
        nc.scalar.dma_start(out=b_row[0:1, C : C + CW], in_=bias_x.rearrange("(o g) -> o g", o=1)[:, 0:CW])
        load_x(0, 0, 512)
        load_x(0, 512, 1024)
        load_a(0)
        load_x(1, 0, 1024)
        load_a(1)
        for h in range(NH):
            for g in range(NG2):
                load_k_half(0, g, h)
        for cw in range(1, NCW):
            for g in range(NG2):
                load_k(cw, g)
        nc.sync.dma_start(out=bx[:, CW:G], in_=bias_x[CW:G].partition_broadcast(P))

        def il_on(eng, dst, src):
            if eng == "v":
                nc.vector.tensor_copy(out=dst, in_=src.rearrange("p j w -> p w j"))
            elif eng == "s":
                nc.scalar.copy(
                    out=dst.rearrange("p (c i) j -> p c j i", i=4), in_=src.rearrange("p j (c i) -> p c j i", i=4)
                )
            else:
                nc.gpsimd.tensor_scalar(
                    out=dst, in0=src.rearrange("p j w -> p w j"), scalar1=1.0, scalar2=0.0, op0=MULT, op1=ADD
                )

        def x_il(b, g, u, eng):
            dst = x_grp[b][:, (2 * g + u) * 256 : (2 * g + u + 1) * 256, :].rearrange("p (q e) j -> p q e j", e=2)
            src = x_raw[b][:, :, g * 512 : (g + 1) * 512].rearrange("p j (q u e) -> p u q e j", u=2, e=2)[:, u, :, :, :]
            if eng == "v":
                nc.vector.tensor_copy(out=dst, in_=src)
            else:
                nc.scalar.copy(out=dst, in_=src)

        def x_q(b, lo, hi):
            nc.vector.quantize_mx(
                out=x_cod[b][:, lo:hi].bitcast(FP8X4),
                scales=x_scl[b][:, lo:hi],
                in_=x_grp[b][:, lo:hi, :].rearrange("p c j -> p (c j)"),
            )

        def spread(dst, lo, turn=False):
            pb = psum.tile([P, 1024], BF16, name="pb", tag="bank")
            for hh in range(2):
                nc.tensor.matmul(
                    out=pb[:, hh * 512 : (hh + 1) * 512],
                    lhsT=ones[:],
                    rhs=b_row[:, lo + hh * 512 : lo + (hh + 1) * 512],
                    start=True,
                    stop=True,
                )
            if turn:
                nc.scalar.copy(
                    out=dst.bitcast(F32).rearrange("p (g u q) -> p g u q", g=NG2, u=2),
                    in_=pb[:].bitcast(F32).rearrange("p (g q u) -> p g u q", g=NG2, u=2),
                )
            else:
                nc.scalar.copy(out=dst, in_=pb[:])

        tr_tiles = {}

        def a_tr(b, s):
            tr = psum.tile([P, 2, 2, P], F32, name="tr", tag="bank")
            tr_tiles[(b, s)] = tr
            for e in range(2):
                words = a_raw[b][:, 2 * s + e, :].bitcast(F32)
                for u in range(2):
                    nc.tensor.transpose(tr[:, e, u, :], words[:, u : N // 2 : 2], ident[:])

        def a_cp(b, s, eng):
            tr = tr_tiles[(b, s)]
            dst = a_grp[b][:, 2 * s * P : (2 * s + 2) * P, :].rearrange("p n t -> p (n t)").bitcast(F32)
            d = dst.rearrange("p (e r u) -> p e r u", e=2, u=2)
            s_ = tr[:].rearrange("p e u r -> p e r u")
            if eng == "v":
                nc.vector.tensor_copy(out=d, in_=s_)
            else:
                nc.scalar.copy(out=d, in_=s_)

        def a_q(b):
            nc.vector.quantize_mx(
                out=a_cod[b][:].bitcast(FP8X4),
                scales=a_scl[b][:],
                in_=a_grp[b][:].rearrange("p n t -> p (n t)"),
            )

        s1_tiles = {}
        vrows = {}
        vt_tiles = {}

        def s1_mm(r):
            b, it = r // NIT, r % NIT
            s1 = psum.tile([P, C], BF16, name="s1", tag="bank")
            s1_tiles[r] = s1
            rows = slice(it * P, (it + 1) * P)
            nc.tensor.matmul_mx(
                out=s1[:],
                lhsT=a_cod[b][:, rows].bitcast(FP8X4),
                lhsT_scale=a_scl[b][:, rows],
                rhs=x_cod[b][:].bitcast(FP8X4),
                rhs_scale=x_scl[b][:],
                start=True,
                stop=True,
            )

        def s1_out(r):
            vrow = vrp.tile([P, C], BF16, name="vrow")
            vrows[r] = vrow
            nc.vector.tensor_tensor(out=vrow[:], in0=s1_tiles[r][:], in1=gcbb[:], op=ADD)

        def v_tr(r):
            vt = psum.tile([P, 2, 2, P], F32, name="vt", tag="bank")
            vt_tiles[r] = vt
            words = vrows[r][:].bitcast(F32)
            for g in range(NG2):
                for u in range(2):
                    nc.tensor.transpose(vt[:, g, u, :], words[:, (2 * g + u) * P : (2 * g + u + 1) * P], ident[:])

        def v_cp(r, eng):
            dst = v_grp[r // VQ][:, r % VQ, :, :, :].rearrange("p g n t -> p (g n t)").bitcast(F32)
            d = dst.rearrange("p (g n u) -> p g n u", g=NG2, u=2)
            s_ = vt_tiles[r][:].rearrange("p g u n -> p g n u")
            if eng == "v":
                nc.vector.tensor_copy(out=d, in_=s_)
            else:
                nc.scalar.copy(out=d, in_=s_)

        def v_q(q):
            nc.vector.quantize_mx(
                out=v_cod[q][:].rearrange("p r g n -> p (r g n)").bitcast(FP8X4),
                scales=v_scl[q][:].rearrange("p r g n -> p (r g n)"),
                in_=v_grp[q][:].rearrange("p r g n t -> p (r g n t)"),
            )

        kg_tiles = {}

        def k_il(c, g, lo, hi, eng):
            if (c, g) not in kg_tiles:
                if g == 0 or c == 0:
                    kg = kgp.tile([P, 512, 4], BF16, name="kg", align_bytes=64)
                else:
                    kg = chain.tile([P, 512, 4], BF16, name="kl", tag="link", align_bytes=64)
                kg_tiles[(c, g)] = kg
            cw, h = c // NH, c % NH
            il_on(eng, kg_tiles[(c, g)][:, lo:hi, :], k_raw[cw][g][:, :, h * 512 + lo : h * 512 + hi])

        def k_q(c, g):
            nc.vector.quantize_mx(
                out=k_cod[c][:, g, :].bitcast(FP8X4),
                scales=k_scl[c][:, g, :],
                in_=kg_tiles[(c, g)][:].rearrange("p w j -> p (w j)"),
            )

        s2_tiles = {}

        def s2_mm(c, r):
            acc = psum.tile([P, 512], F32, name="acc", tag="bank")
            s2_tiles[(c, r)] = acc
            for g in range(NG2):
                nc.tensor.matmul_mx(
                    out=acc[:],
                    lhsT=v_cod[r // VQ][:, r % VQ, g, :].bitcast(FP8X4),
                    lhsT_scale=v_scl[r // VQ][:, r % VQ, g, :],
                    rhs=k_cod[c][:, g, :].bitcast(FP8X4),
                    rhs_scale=k_scl[c][:, g, :],
                    start=(g == 0),
                    stop=(g == NG2 - 1),
                )

        o_tiles = {}

        def o_half(c, r):
            if (c, r // 2) not in o_tiles:
                o_tiles[(c, r // 2)] = osb.tile([P, 2, 512], F32, name="o")
            return o_tiles[(c, r // 2)][:, r % 2, :]

        def store2(c, r):
            b, it = r // NIT, r % NIT
            nc.sync.dma_start(out=out_v[b, :, it : it + 2, c * 512 : (c + 1) * 512], in_=o_tiles[(c, r // 2)][:])

        def store1(c, r):
            b, it = r // NIT, r % NIT
            nc.sync.dma_start(out=out_v[b, :, it, c * 512 : (c + 1) * 512], in_=o_half(c, r))

        def s2_out(c, r):
            nc.vector.tensor_tensor(out=o_half(c, r), in0=s2_tiles[(c, r)][:], in1=bx[:, c * 512 : (c + 1) * 512], op=ADD)
            if c == NCH - 1 and r >= NRT - 2:
                store1(c, r)
            elif r % 2 == 1 and not (r == 1 and c >= 1):
                store2(c, r - 1)

        def s2_side(c, r):
            sums = sidep.tile([P, 512], F32, name="sums")
            nc.scalar.copy(out=sums[:], in_=s2_tiles[(c, r)][:])
            nc.gpsimd.tensor_tensor(out=o_half(c, r), in0=sums[:], in1=bx[:, c * 512 : (c + 1) * 512], op=ADD)

        x_il(0, 0, 0, "v")
        x_il(0, 0, 1, "v")
        x_q(0, 0, 512)
        x_il(0, 1, 1, "s")
        x_il(0, 1, 0, "v")
        a_tr(0, 0)
        a_tr(0, 1)
        a_cp(0, 0, "s")
        a_cp(0, 1, "s")
        spread(gcbb[:], 0, turn=True)
        x_q(0, 512, 1024)
        a_q(0)
        for r in range(4):
            s1_mm(r)
        x_il(1, 0, 0, "v")
        x_il(1, 0, 1, "v")
        x_il(1, 1, 0, "s")
        x_il(1, 1, 1, "s")
        a_tr(1, 0)
        a_tr(1, 1)
        a_cp(1, 0, "s")
        a_cp(1, 1, "s")
        s1_out(0)
        s1_out(1)
        v_tr(0)
        v_tr(1)
        x_q(1, 0, 1024)
        s1_out(2)
        s1_out(3)
        a_q(1)
        v_tr(2)
        v_tr(3)
        for r in range(4, 8):
            s1_mm(r)
        k_il(0, 0, 0, 512, "s")
        k_il(0, 1, 0, 512, "v")
        for r in range(4):
            v_cp(r, "s")
        for r in range(4, 8):
            s1_out(r)
            v_tr(r)
        v_q(0)
        k_q(0, 0)
        k_q(0, 1)
        for r in range(4, 8):
            v_cp(r, "s")
        spread(bx[:, 0:CW], C)
        k_il(1, 0, 0, 512, "s")

        banks = [(c, r) for c in range(NCH) for r in range(NRT)]
        AHEAD = 3
        QPOS = 5
        for i in range(AHEAD):
            s2_mm(banks[i][0], banks[i][1])
        GW = 256

        v_q(1)
        k_il(1, 1, 512 - GW, 512, "g")
        k_il(1, 1, 0, 512 - GW, "s")
        k_il(2, 0, 0, 512, "s")
        for i in range(len(banks)):
            c, r = banks[i]
            if r == QPOS and c >= 1:
                store2(c, 0)
            if r == QPOS and c + 1 < NCH:
                k_q(c + 1, 0)
                k_q(c + 1, 1)
                if c + 2 < NCH:
                    k_il(c + 2, 1, 512 - GW, 512, "g")
            if i + AHEAD < len(banks):
                s2_mm(banks[i + AHEAD][0], banks[i + AHEAD][1])
            if r == 0 and c >= 1:
                s2_side(c, r)
                if c + 1 < NCH:
                    k_il(c + 1, 1, 0, 512 - GW, "s")
                if c + 2 < NCH:
                    k_il(c + 2, 0, 0, 512, "s")
            else:
                s2_out(c, r)
